import numpy as np
import ml_dtypes


def mxq(x, axis, fmt="e4m3"):
    dtype, down = {"e4m3": (ml_dtypes.float8_e4m3fn, 7), "e5m2": (ml_dtypes.float8_e5m2, 14)}[fmt]
    v = np.moveaxis(np.asarray(x, np.float32).astype(ml_dtypes.bfloat16).astype(np.float64), axis, -1)
    blocks = v.reshape(v.shape[:-1] + (-1, 32))
    amax = np.abs(blocks).max(-1, keepdims=True)
    byte = np.maximum(np.where(amax > 0, np.frexp(amax)[1] - 1 + 127, 0) - down, 1)
    scale = np.exp2(byte - 127.0)
    codes = (blocks / scale).astype(np.float32).astype(dtype).astype(np.float64)
    return np.moveaxis((codes * scale).reshape(v.shape), -1, axis)


WIDE = False


def mx_kscale(k):
    if not WIDE:
        return np.ones(k)
    levels = np.array([10, -10, 5, -5, 0])
    if k % 512:
        return np.exp2(np.random.permutation(np.resize(levels, k // 32))).repeat(32)
    a = np.empty((k // 512, 16))
    for p in range(k // 512):
        a[p, :8] = np.random.permutation(np.resize(levels, 8))
        for g in range(8):
            far = levels[np.abs(levels - a[p, g]) >= 10]
            a[p, g + 8] = far[np.random.randint(len(far))]
    return np.exp2(a.ravel()).repeat(32)


BF16 = ml_dtypes.bfloat16


def bf(x):
    return np.asarray(x, np.float32).astype(BF16)


def f64(x):
    return np.asarray(x).astype(np.float64)


B, S, V, E, M = 512, 16, 4096, 512, 1024


def setup_inputs():
    s, t = mx_kscale(E), mx_kscale(M)
    return {"y2": bf(np.maximum(np.random.standard_normal((B, E)), 0.0) * s),
            "first": bf(np.random.standard_normal((B, M)) * 0.4 * t),
            "w_second": bf(np.random.standard_normal((M, E)) * 1.4 / np.sqrt(E) / s[None, :]),
            "b_second": bf(np.random.standard_normal(M) * 0.3),
            "w_int": bf(np.random.standard_normal((M, E)) * 1.4 / np.sqrt(E) / s[None, :] * t[:, None]),
            "b_int": bf(np.random.standard_normal(M) * 0.3 * t),
            "w_out": bf(np.random.standard_normal((V, M)) / np.sqrt(M) / t[None, :]),
            "b_out": bf(np.random.standard_normal(V) * 0.3)}


def reference(y2, first, w_second, b_second, w_int, b_int, w_out, b_out):
    y2q = mxq(f64(y2), 1, "e4m3")
    second = np.maximum((y2q @ mxq(f64(w_second), 1, "e4m3").T) + f64(b_second), 0.0)
    inter = np.maximum((y2q @ mxq(f64(w_int), 1, "e4m3").T) + f64(b_int), 0.0)
    z = second * f64(first) + inter
    return (mxq(z, 1, "e4m3") @ mxq(f64(w_out), 1, "e4m3").T) + f64(b_out)

@@ -1,0 +1,260 @@
+from contextlib import ExitStack
+
+import concourse.mybir as mybir
+from concourse.masks import make_identity
+
+B, E, M, V = 512, 512, 1024, 4096
+FLOPS = 2 * B * E * M * 2 + 2 * B * M * V
+
+F32 = mybir.dt.float32
+BF16 = mybir.dt.bfloat16
+U32 = mybir.dt.uint32
+U8 = mybir.dt.uint8
+FP8X4 = mybir.dt.float8_e4m3fn_x4
+ACT = mybir.ActivationFunctionType
+ALU = mybir.AluOpType
+
+P = 128
+BANK_DT = F32
+CHUNK = 512
+N_CHUNKS = V // CHUNK
+AHEAD = 4
+PP_FROM = 8
+PP_VEC_J = 3
+PP_LEAD = 1
+
+
+def tile_smcrossbaby_1_pb_kernel(tc, y2, first, w_second, b_second, w_int, b_int, w_out, b_out, out):
+    nc = tc.nc
+    with ExitStack() as ctx:
+        const = ctx.enter_context(tc.tile_pool(name="const", bufs=1))
+        raw = ctx.enter_context(tc.tile_pool(name="raw", bufs=8))
+        grp = ctx.enter_context(tc.tile_pool(name="grp", bufs=4))
+        keep = ctx.enter_context(tc.tile_pool(name="keep", bufs=1))
+        wcod = ctx.enter_context(tc.tile_pool(name="wcod", bufs=AHEAD + 1))
+        mid = ctx.enter_context(tc.tile_pool(name="mid", bufs=2))
+        perm = ctx.enter_context(tc.tile_pool(name="perm", bufs=8))
+        outp = ctx.enter_context(tc.tile_pool(name="outp", bufs=6))
+        psum = ctx.enter_context(tc.psum_pool(name="psum", bufs=8))
+        ctx.enter_context(tc.manual_schedule(engines={mybir.EngineType.PE}))
+
+        bcol = const.tile([P, 2, 2, 4], F32, name="bcol")
+        for which, vec in enumerate((b_second, b_int)):
+            bcol_raw = const.tile([P, 2, 4], BF16, name="bcol_raw%d" % which)
+            nc.scalar.dma_start(out=bcol_raw[:], in_=vec.rearrange("(g p t) -> p g t", g=2, t=4))
+            nc.vector.tensor_copy(out=bcol[:, which, :, :], in_=bcol_raw[:])
+        y_raw = raw.tile([P, 4, E], BF16, tag="raw", name="y_raw")
+        y_view = y2.rearrange("(a p) k -> p a k", p=P)
+        nc.sync.dma_start(out=y_raw[:, 0:2, :], in_=y_view[:, 0:2, :])
+        nc.sync.dma_start(out=y_raw[:, 2:4, :], in_=y_view[:, 2:4, :])
+        ws_raw = raw.tile([P, 2, 4, E], BF16, tag="raw", name="ws_raw")
+        wi_raw = raw.tile([P, 2, 4, E], BF16, tag="raw", name="wi_raw")
+        f_raw = raw.tile([P, 2, 4, 512], BF16, tag="raw", name="f_raw")
+        for g in range(2):
+            rows = slice(512 * g, 512 * (g + 1))
+            nc.sync.dma_start(out=ws_raw[:, g, :, :], in_=w_second[rows, :].rearrange("(m t) k -> m t k", t=4))
+            nc.sync.dma_start(out=wi_raw[:, g, :, :], in_=w_int[rows, :].rearrange("(m t) k -> m t k", t=4))
+        for g in range(2):
+            rows = slice(512 * g, 512 * (g + 1))
+            nc.sync.dma_start(out=f_raw[:, g, :, :], in_=first[:, rows].rearrange("(a p) c -> p a c", p=P))
+        bias_bc = const.tile([P, V], BF16, name="bias_bc")
+
+        def load_bias(c):
+            vcols = slice(CHUNK * c, CHUNK * (c + 1))
+            nc.sync.dma_start(out=bias_bc[:, vcols], in_=b_out[vcols].partition_broadcast(P))
+
+        wo_raw = []
+        for c in range(N_CHUNKS):
+            t_raw = raw.tile([P, 4, M], BF16, tag="raw", name="wo_raw")
+            nc.sync.dma_start(out=t_raw[:], in_=w_out[CHUNK * c : CHUNK * (c + 1), :].rearrange("(j p) k -> p j k", p=P))
+            wo_raw.append(t_raw)
+            if c >= 2:
+                load_bias(c - 2)
+        load_bias(N_CHUNKS - 2)
+        load_bias(N_CHUNKS - 1)
+
+        ident = const.tile([P, P], F32, name="ident")
+        make_identity(nc, ident[:])
+        warm = const.tile([P, 1], F32, name="warm")
+        nc.vector.memset(warm[:], 0.0)
+        warm2 = const.tile([P, 1], F32, name="warm2")
+        nc.scalar.activation(out=warm2[:], in_=warm[:], func=ACT.Relu)
+
+        def turn(srcs):
+            xt = psum.tile([P, 2, 2, P], F32, tag="bank", name="xt")
+            for x in range(2):
+                words = srcs[x].bitcast(F32)
+                for u in range(2):
+                    nc.tensor.transpose(xt[:, x, u, :], words[:, u::2], ident[:])
+            return xt
+
+        def empty(xt, dst_words):
+            nc.scalar.copy(out=dst_words, in_=xt[:].rearrange("p x u r -> p x r u"))
+
+        def quantize(grouped_flat, width, pool, label):
+            codes = pool.tile([P, width // 4], U32, name=label + "_c", tag=label + "_c", align_bytes=64)
+            scales = pool.tile([P, width // 4], U8, name=label + "_s", tag=label + "_s", align_bytes=64)
+            nc.vector.quantize_mx(out=codes[:].bitcast(FP8X4), scales=scales[:], in_=grouped_flat)
+            return codes, scales
+
+        def turn_w(w_raw, g):
+            w_g = grp.tile([P, 4, P, 4], BF16, tag="grp", name="w_g", align_bytes=64)
+            for b in range(2):
+                empty(turn([w_raw[:, g, 2 * b, :], w_raw[:, g, 2 * b + 1, :]]), w_g[:, 2 * b : 2 * b + 2, :, :].bitcast(F32))
+            return w_g
+
+        def quant_w(w_g, label):
+            return quantize(w_g[:].rearrange("p t m j -> p (t m j)"), 2048, keep, label)
+
+        def turn_f(g):
+            return [turn([f_raw[:, g, 2 * b, :], f_raw[:, g, 2 * b + 1, :]]) for b in range(2)]
+
+        def stage1(g, which, w_q, dst):
+            codes, scales = w_q
+            for t in range(4):
+                ps = psum.tile([P, B], BANK_DT, tag="bank", name="ps1")
+                cols = slice(P * t, P * (t + 1))
+                nc.tensor.matmul_mx(
+                    out=ps[:],
+                    lhsT=codes[:, cols].bitcast(FP8X4),
+                    lhsT_scale=scales[:, cols],
+                    rhs=y_c[:].bitcast(FP8X4),
+                    rhs_scale=y_s[:],
+                    start=True,
+                    stop=True,
+                )
+                b_ap = bcol[:, which, g, t : t + 1]
+                if g == 0 and which == 1 and t % 2 == 0:
+                    nc.vector.tensor_scalar(out=dst[:, t, :], in0=ps[:], scalar1=b_ap, scalar2=0.0, op0=ALU.add, op1=ALU.max)
+                else:
+                    nc.scalar.activation(out=dst[:, t, :], in_=ps[:], func=ACT.Relu, bias=b_ap, scale=1.0)
+
+        def gate_mul(s_sb, f_banks):
+            prods = []
+            for h in range(2):
+                sf = mid.tile([P, 256, 4], F32, tag="sf", name="sf")
+                for x in range(2):
+                    toks = slice(256 * h + P * x, 256 * h + P * (x + 1))
+                    nc.vector.tensor_tensor(
+                        out=sf[:, P * x : P * (x + 1), :].rearrange("p r (u e) -> p r u e", e=2),
+                        in0=s_sb[:, :, toks].rearrange("p (u e) r -> p r u e", e=2),
+                        in1=f_banks[h][:, x, :, :].bitcast(BF16).rearrange("p u (r e) -> p r u e", e=2),
+                        op=ALU.mult,
+                    )
+                prods.append(sf)
+            return prods
+
+        def gate_add(prods, i_sb):
+            z_g = mid.tile([P, B, 4], BF16, tag="z_g", name="z_g", align_bytes=64)
+            for h in range(2):
+                toks = slice(256 * h, 256 * (h + 1))
+                nc.vector.tensor_tensor(out=z_g[:, toks, :], in0=prods[h][:], in1=i_sb[:, :, toks].rearrange("p t n -> p n t"), op=ALU.add)
+            return z_g
+
+        def quant_z(z_g, label):
+            codes = keep.tile([P, B], U32, name=label + "_c", align_bytes=64)
+            scales = keep.tile([P, B], U8, name=label + "_s", align_bytes=64)
+            for h in range(2):
+                toks = slice(256 * h, 256 * (h + 1))
+                nc.vector.quantize_mx(
+                    out=codes[:, toks].bitcast(FP8X4), scales=scales[:, toks], in_=z_g[:, toks, :].rearrange("p n t -> p (n t)")
+                )
+            return codes, scales
+
+        sorted_words = {}
+
+        def sort_words(c):
+            if c < PP_FROM or c >= N_CHUNKS:
+                return
+            for j in range(4):
+                pw = perm.tile([P, 2, 2, P], F32, tag="pw", name="pw")
+                src = wo_raw[c][:, j, :].bitcast(F32).rearrange("p (g w u) -> p g u w", g=2, u=2)
+                if j >= PP_VEC_J:
+                    nc.vector.tensor_copy(out=pw[:], in_=src)
+                else:
+                    nc.scalar.copy(out=pw[:], in_=src)
+                sorted_words[(c, j)] = pw
+
+        def turn_wo(c):
+            wo_g = grp.tile([P, 2, CHUNK, 4], BF16, tag="grp", name="wo_g", align_bytes=64)
+            for j in range(4):
+                if c >= PP_FROM:
+                    pw = sorted_words[(c, j)]
+                    xt = psum.tile([P, 2, 2, P], F32, tag="bank", name="xt")
+                    for g in range(2):
+                        for u in range(2):
+                            nc.tensor.transpose(xt[:, g, u, :], pw[:, g, u, :], ident[:])
+                else:
+                    xt = turn([wo_raw[c][:, j, 0:512], wo_raw[c][:, j, 512:1024]])
+                empty(xt, wo_g[:, :, P * j : P * (j + 1), :].bitcast(F32))
+            return wo_g
+
+        def quant_wo(wo_g):
+            return quantize(wo_g[:].rearrange("p g v t -> p (g v t)"), 8 * CHUNK, wcod, "wo")
+
+        def stage2(c, wo_q):
+            codes, scales = wo_q
+            for m in range(4):
+                acc = psum.tile([P, CHUNK], F32, tag="bank", name="acc")
+                toks = slice(P * m, P * (m + 1))
+                for g in range(2):
+                    cols = slice(CHUNK * g, CHUNK * (g + 1))
+                    nc.tensor.matmul_mx(
+                        out=acc[:],
+                        lhsT=z_q[g][0][:, toks].bitcast(FP8X4),
+                        lhsT_scale=z_q[g][1][:, toks],
+                        rhs=codes[:, cols].bitcast(FP8X4),
+                        rhs_scale=scales[:, cols],
+                        start=(g == 0),
+                        stop=(g == 1),
+                    )
+                o_sb = outp.tile([P, CHUNK], F32, tag="o_sb", name="o_sb")
+                vcols = slice(CHUNK * c, CHUNK * (c + 1))
+                nc.vector.tensor_tensor(out=o_sb[:], in0=acc[:], in1=bias_bc[:, vcols], op=ALU.add)
+                nc.sync.dma_start(out=out[toks, vcols], in_=o_sb[:])
+
+        y_g = grp.tile([P, B, 4], BF16, tag="grp", name="y_g", align_bytes=64)
+        for b in range(2):
+            empty(
+                turn([y_raw[:, 2 * b, :], y_raw[:, 2 * b + 1, :]]),
+                y_g[:, 256 * b : 256 * (b + 1), :].bitcast(F32).rearrange("p (x r) u -> p x r u", x=2),
+            )
+        y_c, y_s = quantize(y_g[:].rearrange("p n t -> p (n t)"), 4 * B, keep, "y")
+
+        ws_g0 = turn_w(ws_raw, 0)
+        wi_g0 = turn_w(wi_raw, 0)
+        ws_q0 = quant_w(ws_g0, "ws0")
+        wi_q0 = quant_w(wi_g0, "wi0")
+        ws_g1 = turn_w(ws_raw, 1)
+        wi_g1 = turn_w(wi_raw, 1)
+        s0 = mid.tile([P, 4, B], F32, tag="s_sb", name="s_sb")
+        i0 = mid.tile([P, 4, B], F32, tag="i_sb", name="i_sb")
+        stage1(0, 0, ws_q0, s0)
+        stage1(0, 1, wi_q0, i0)
+        f_banks0 = turn_f(0)
+        ws_q1 = quant_w(ws_g1, "ws1")
+        wi_q1 = quant_w(wi_g1, "wi1")
+        prods0 = gate_mul(s0, f_banks0)
+        wo_qs = {}
+        sort_words(0)
+        wo_g0 = turn_wo(0)
+        s1 = mid.tile([P, 4, B], F32, tag="s_sb", name="s_sb")
+        i1 = mid.tile([P, 4, B], F32, tag="i_sb", name="i_sb")
+        stage1(1, 0, ws_q1, s1)
+        stage1(1, 1, wi_q1, i1)
+        f_banks1 = turn_f(1)
+        z_g0 = gate_add(prods0, i0)
+        prods1 = gate_mul(s1, f_banks1)
+        z_q = [quant_z(z_g0, "z0")]
+        z_g1 = gate_add(prods1, i1)
+        z_q.append(quant_z(z_g1, "z1"))
+        wo_qs[0] = quant_wo(wo_g0)
+        for c in range(1, AHEAD + PP_LEAD):
+            sort_words(c)
+        for c in range(1, AHEAD):
+            wo_qs[c] = quant_wo(turn_wo(c))
+        for c in range(N_CHUNKS):
+            sort_words(c + AHEAD + PP_LEAD)
+            stage2(c, wo_qs[c])
+            if c + AHEAD < N_CHUNKS:
+                wo_qs[c + AHEAD] = quant_wo(turn_wo(c + AHEAD))

@@ -18,10 +18,9 @@ P = 128
 BANK_DT = F32
 CHUNK = 512
 N_CHUNKS = V // CHUNK
-AHEAD = 4
-PP_FROM = 8
-PP_VEC_J = 3
-PP_LEAD = 1
+AHEAD = 3
+SORT_FROM = 3
+WARM = 6
 
 
 def tile_smcrossbaby_1_pb_kernel(tc, y2, first, w_second, b_second, w_int, b_int, w_out, b_out, out):
@@ -65,8 +64,8 @@ def tile_smcrossbaby_1_pb_kernel(tc, y2, first, w_second, b_second, w_int, b_int
 
         wo_raw = []
         for c in range(N_CHUNKS):
-            t_raw = raw.tile([P, 4, M], BF16, tag="raw", name="wo_raw")
-            nc.sync.dma_start(out=t_raw[:], in_=w_out[CHUNK * c : CHUNK * (c + 1), :].rearrange("(j p) k -> p j k", p=P))
+            t_raw = raw.tile([P, 4, 2, 512], BF16, tag="raw", name="wo_raw")
+            nc.sync.dma_start(out=t_raw[:], in_=w_out[CHUNK * c : CHUNK * (c + 1), :].rearrange("(j p) (x k) -> p j x k", p=P, x=2))
             wo_raw.append(t_raw)
             if c >= 2:
                 load_bias(c - 2)
@@ -79,14 +78,35 @@ def tile_smcrossbaby_1_pb_kernel(tc, y2, first, w_second, b_second, w_int, b_int
         nc.vector.memset(warm[:], 0.0)
         warm2 = const.tile([P, 1], F32, name="warm2")
         nc.scalar.activation(out=warm2[:], in_=warm[:], func=ACT.Relu)
+        if WARM > 0:
+            zeros = const.tile([P, 512], BF16, name="zeros")
+            nc.gpsimd.memset(zeros[:], 0.0)
+            idle = psum.tile([P, 512], F32, tag="bank", name="idle")
+            for i in range(WARM):
+                nc.tensor.matmul(idle[:], lhsT=zeros[:, 0:P], rhs=zeros[:], start=True, stop=True)
 
-        def turn(srcs):
+        def sort_words(pair, on_vector):
+            pw = perm.tile([P, 2, 2, P], F32, tag="pw", name="pw")
+            src = pair.bitcast(F32).rearrange("p x (w u) -> p x u w", u=2)
+            if on_vector:
+                nc.vector.tensor_copy(out=pw[:], in_=src)
+            else:
+                nc.scalar.copy(out=pw[:], in_=src)
+            return pw
+
+        def turn(pair, pw=None):
             xt = psum.tile([P, 2, 2, P], F32, tag="bank", name="xt")
+            words = pair.bitcast(F32)
             for x in range(2):
-                words = srcs[x].bitcast(F32)
                 for u in range(2):
-                    nc.tensor.transpose(xt[:, x, u, :], words[:, u::2], ident[:])
+                    if pw is None:
+                        nc.tensor.transpose(xt[:, x, u, :], words[:, x, u::2], ident[:])
+                    else:
+                        nc.tensor.transpose(xt[:, x, u, :], pw[:, x, u, :], ident[:])
             return xt
+
+        def turn_head(pair):
+            return turn(pair, sort_words(pair, True))
 
         def empty(xt, dst_words):
             nc.scalar.copy(out=dst_words, in_=xt[:].rearrange("p x u r -> p x r u"))
@@ -100,14 +120,14 @@ def tile_smcrossbaby_1_pb_kernel(tc, y2, first, w_second, b_second, w_int, b_int
         def turn_w(w_raw, g):
             w_g = grp.tile([P, 4, P, 4], BF16, tag="grp", name="w_g", align_bytes=64)
             for b in range(2):
-                empty(turn([w_raw[:, g, 2 * b, :], w_raw[:, g, 2 * b + 1, :]]), w_g[:, 2 * b : 2 * b + 2, :, :].bitcast(F32))
+                empty(turn_head(w_raw[:, g, 2 * b : 2 * b + 2, :]), w_g[:, 2 * b : 2 * b + 2, :, :].bitcast(F32))
             return w_g
 
         def quant_w(w_g, label):
             return quantize(w_g[:].rearrange("p t m j -> p (t m j)"), 2048, keep, label)
 
         def turn_f(g):
-            return [turn([f_raw[:, g, 2 * b, :], f_raw[:, g, 2 * b + 1, :]]) for b in range(2)]
+            return [turn_head(f_raw[:, g, 2 * b : 2 * b + 2, :]) for b in range(2)]
 
         def stage1(g, which, w_q, dst):
             codes, scales = w_q
@@ -161,31 +181,16 @@ def tile_smcrossbaby_1_pb_kernel(tc, y2, first, w_second, b_second, w_int, b_int
                 )
             return codes, scales
 
-        sorted_words = {}
+        sorted_wo = {}
 
-        def sort_words(c):
-            if c < PP_FROM or c >= N_CHUNKS:
-                return
-            for j in range(4):
-                pw = perm.tile([P, 2, 2, P], F32, tag="pw", name="pw")
-                src = wo_raw[c][:, j, :].bitcast(F32).rearrange("p (g w u) -> p g u w", g=2, u=2)
-                if j >= PP_VEC_J:
-                    nc.vector.tensor_copy(out=pw[:], in_=src)
-                else:
-                    nc.scalar.copy(out=pw[:], in_=src)
-                sorted_words[(c, j)] = pw
+        def sort_wo(c):
+            if SORT_FROM <= c < N_CHUNKS:
+                sorted_wo[c] = [sort_words(wo_raw[c][:, j, :, :], j >= 3) for j in range(4)]
 
         def turn_wo(c):
             wo_g = grp.tile([P, 2, CHUNK, 4], BF16, tag="grp", name="wo_g", align_bytes=64)
             for j in range(4):
-                if c >= PP_FROM:
-                    pw = sorted_words[(c, j)]
-                    xt = psum.tile([P, 2, 2, P], F32, tag="bank", name="xt")
-                    for g in range(2):
-                        for u in range(2):
-                            nc.tensor.transpose(xt[:, g, u, :], pw[:, g, u, :], ident[:])
-                else:
-                    xt = turn([wo_raw[c][:, j, 0:512], wo_raw[c][:, j, 512:1024]])
+                xt = turn(wo_raw[c][:, j, :, :], sorted_wo[c][j] if c in sorted_wo else None)
                 empty(xt, wo_g[:, :, P * j : P * (j + 1), :].bitcast(F32))
             return wo_g
 
@@ -216,7 +221,7 @@ def tile_smcrossbaby_1_pb_kernel(tc, y2, first, w_second, b_second, w_int, b_int
         y_g = grp.tile([P, B, 4], BF16, tag="grp", name="y_g", align_bytes=64)
         for b in range(2):
             empty(
-                turn([y_raw[:, 2 * b, :], y_raw[:, 2 * b + 1, :]]),
+                turn_head(y_raw[:, 2 * b : 2 * b + 2, :]),
                 y_g[:, 256 * b : 256 * (b + 1), :].bitcast(F32).rearrange("p (x r) u -> p x r u", x=2),
             )
         y_c, y_s = quantize(y_g[:].rearrange("p n t -> p (n t)"), 4 * B, keep, "y")
@@ -236,7 +241,7 @@ def tile_smcrossbaby_1_pb_kernel(tc, y2, first, w_second, b_second, w_int, b_int
         wi_q1 = quant_w(wi_g1, "wi1")
         prods0 = gate_mul(s0, f_banks0)
         wo_qs = {}
-        sort_words(0)
+        sort_wo(0)
         wo_g0 = turn_wo(0)
         s1 = mid.tile([P, 4, B], F32, tag="s_sb", name="s_sb")
         i1 = mid.tile([P, 4, B], F32, tag="i_sb", name="i_sb")
@@ -249,12 +254,12 @@ def tile_smcrossbaby_1_pb_kernel(tc, y2, first, w_second, b_second, w_int, b_int
         z_g1 = gate_add(prods1, i1)
         z_q.append(quant_z(z_g1, "z1"))
         wo_qs[0] = quant_wo(wo_g0)
-        for c in range(1, AHEAD + PP_LEAD):
-            sort_words(c)
+        for c in range(1, AHEAD + 1):
+            sort_wo(c)
         for c in range(1, AHEAD):
             wo_qs[c] = quant_wo(turn_wo(c))
         for c in range(N_CHUNKS):
-            sort_words(c + AHEAD + PP_LEAD)
+            sort_wo(c + AHEAD + 1)
             stage2(c, wo_qs[c])
             if c + AHEAD < N_CHUNKS:
                 wo_qs[c + AHEAD] = quant_wo(turn_wo(c + AHEAD))

@@ -15,12 +15,18 @@ ACT = mybir.ActivationFunctionType
 ALU = mybir.AluOpType
 
 P = 128
-BANK_DT = F32
+PACK = 4
+K_PASS = P * PACK
+PASSES = M // K_PASS
+STAGE1_PSUM_DT = F32
 CHUNK = 512
 N_CHUNKS = V // CHUNK
-AHEAD = 3
-SORT_FROM = 3
-WARM = 6
+ROW_TILES = CHUNK // P
+TOK_TILES = B // P
+TOK_HALF = B // 2
+AHEAD = 4
+SHARED_FROM = N_CHUNKS - AHEAD
+SHARED_TILE = 1
 
 
 def tile_smcrossbaby_1_pb_kernel(tc, y2, first, w_second, b_second, w_int, b_int, w_out, b_out, out):
@@ -32,30 +38,29 @@ def tile_smcrossbaby_1_pb_kernel(tc, y2, first, w_second, b_second, w_int, b_int
         keep = ctx.enter_context(tc.tile_pool(name="keep", bufs=1))
         wcod = ctx.enter_context(tc.tile_pool(name="wcod", bufs=AHEAD + 1))
         mid = ctx.enter_context(tc.tile_pool(name="mid", bufs=2))
-        perm = ctx.enter_context(tc.tile_pool(name="perm", bufs=8))
-        outp = ctx.enter_context(tc.tile_pool(name="outp", bufs=6))
+        outp = ctx.enter_context(tc.tile_pool(name="outp", bufs=12))
         psum = ctx.enter_context(tc.psum_pool(name="psum", bufs=8))
         ctx.enter_context(tc.manual_schedule(engines={mybir.EngineType.PE}))
 
-        bcol = const.tile([P, 2, 2, 4], F32, name="bcol")
+        bcol = const.tile([P, 2, PASSES, PACK], F32, name="bcol")
         for which, vec in enumerate((b_second, b_int)):
-            bcol_raw = const.tile([P, 2, 4], BF16, name="bcol_raw%d" % which)
-            nc.scalar.dma_start(out=bcol_raw[:], in_=vec.rearrange("(g p t) -> p g t", g=2, t=4))
+            bcol_raw = const.tile([P, PASSES, PACK], BF16, name="bcol_raw%d" % which)
+            nc.scalar.dma_start(out=bcol_raw[:], in_=vec.rearrange("(g p t) -> p g t", g=PASSES, t=PACK))
             nc.vector.tensor_copy(out=bcol[:, which, :, :], in_=bcol_raw[:])
-        y_raw = raw.tile([P, 4, E], BF16, tag="raw", name="y_raw")
+        y_raw = raw.tile([P, TOK_TILES, E], BF16, tag="raw", name="y_raw")
         y_view = y2.rearrange("(a p) k -> p a k", p=P)
         nc.sync.dma_start(out=y_raw[:, 0:2, :], in_=y_view[:, 0:2, :])
         nc.sync.dma_start(out=y_raw[:, 2:4, :], in_=y_view[:, 2:4, :])
-        ws_raw = raw.tile([P, 2, 4, E], BF16, tag="raw", name="ws_raw")
-        wi_raw = raw.tile([P, 2, 4, E], BF16, tag="raw", name="wi_raw")
-        f_raw = raw.tile([P, 2, 4, 512], BF16, tag="raw", name="f_raw")
-        for g in range(2):
-            rows = slice(512 * g, 512 * (g + 1))
-            nc.sync.dma_start(out=ws_raw[:, g, :, :], in_=w_second[rows, :].rearrange("(m t) k -> m t k", t=4))
-            nc.sync.dma_start(out=wi_raw[:, g, :, :], in_=w_int[rows, :].rearrange("(m t) k -> m t k", t=4))
-        for g in range(2):
-            rows = slice(512 * g, 512 * (g + 1))
-            nc.sync.dma_start(out=f_raw[:, g, :, :], in_=first[:, rows].rearrange("(a p) c -> p a c", p=P))
+        ws_raw = raw.tile([P, PASSES, PACK, E], BF16, tag="raw", name="ws_raw")
+        wi_raw = raw.tile([P, PASSES, PACK, E], BF16, tag="raw", name="wi_raw")
+        f_raw = raw.tile([P, PASSES, TOK_TILES, K_PASS], BF16, tag="raw", name="f_raw")
+        for g in range(PASSES):
+            rows = slice(K_PASS * g, K_PASS * (g + 1))
+            nc.sync.dma_start(out=ws_raw[:, g, :, :], in_=w_second[rows, :].rearrange("(m t) k -> m t k", t=PACK))
+            nc.sync.dma_start(out=wi_raw[:, g, :, :], in_=w_int[rows, :].rearrange("(m t) k -> m t k", t=PACK))
+        for g in range(PASSES):
+            chans = slice(K_PASS * g, K_PASS * (g + 1))
+            nc.sync.dma_start(out=f_raw[:, g, :, :], in_=first[:, chans].rearrange("(a p) c -> p a c", p=P))
         bias_bc = const.tile([P, V], BF16, name="bias_bc")
 
         def load_bias(c):
@@ -64,9 +69,9 @@ def tile_smcrossbaby_1_pb_kernel(tc, y2, first, w_second, b_second, w_int, b_int
 
         wo_raw = []
         for c in range(N_CHUNKS):
-            t_raw = raw.tile([P, 4, 2, 512], BF16, tag="raw", name="wo_raw")
-            nc.sync.dma_start(out=t_raw[:], in_=w_out[CHUNK * c : CHUNK * (c + 1), :].rearrange("(j p) (x k) -> p j x k", p=P, x=2))
-            wo_raw.append(t_raw)
+            chunk_raw = raw.tile([P, ROW_TILES, M], BF16, tag="raw", name="wo_raw")
+            nc.sync.dma_start(out=chunk_raw[:], in_=w_out[CHUNK * c : CHUNK * (c + 1), :].rearrange("(j p) k -> p j k", p=P))
+            wo_raw.append(chunk_raw)
             if c >= 2:
                 load_bias(c - 2)
         load_bias(N_CHUNKS - 2)
@@ -78,66 +83,45 @@ def tile_smcrossbaby_1_pb_kernel(tc, y2, first, w_second, b_second, w_int, b_int
         nc.vector.memset(warm[:], 0.0)
         warm2 = const.tile([P, 1], F32, name="warm2")
         nc.scalar.activation(out=warm2[:], in_=warm[:], func=ACT.Relu)
-        if WARM > 0:
-            zeros = const.tile([P, 512], BF16, name="zeros")
-            nc.gpsimd.memset(zeros[:], 0.0)
-            idle = psum.tile([P, 512], F32, tag="bank", name="idle")
-            for i in range(WARM):
-                nc.tensor.matmul(idle[:], lhsT=zeros[:, 0:P], rhs=zeros[:], start=True, stop=True)
 
-        def sort_words(pair, on_vector):
-            pw = perm.tile([P, 2, 2, P], F32, tag="pw", name="pw")
-            src = pair.bitcast(F32).rearrange("p x (w u) -> p x u w", u=2)
-            if on_vector:
-                nc.vector.tensor_copy(out=pw[:], in_=src)
-            else:
-                nc.scalar.copy(out=pw[:], in_=src)
-            return pw
-
-        def turn(pair, pw=None):
+        def turn(srcs):
             xt = psum.tile([P, 2, 2, P], F32, tag="bank", name="xt")
-            words = pair.bitcast(F32)
             for x in range(2):
+                words = srcs[x].bitcast(F32)
                 for u in range(2):
-                    if pw is None:
-                        nc.tensor.transpose(xt[:, x, u, :], words[:, x, u::2], ident[:])
-                    else:
-                        nc.tensor.transpose(xt[:, x, u, :], pw[:, x, u, :], ident[:])
+                    nc.tensor.transpose(xt[:, x, u, :], words[:, u::2], ident[:])
             return xt
-
-        def turn_head(pair):
-            return turn(pair, sort_words(pair, True))
 
         def empty(xt, dst_words):
             nc.scalar.copy(out=dst_words, in_=xt[:].rearrange("p x u r -> p x r u"))
 
         def quantize(grouped_flat, width, pool, label):
-            codes = pool.tile([P, width // 4], U32, name=label + "_c", tag=label + "_c", align_bytes=64)
-            scales = pool.tile([P, width // 4], U8, name=label + "_s", tag=label + "_s", align_bytes=64)
+            codes = pool.tile([P, width // PACK], U32, name=label + "_c", tag=label + "_c", align_bytes=64)
+            scales = pool.tile([P, width // PACK], U8, name=label + "_s", tag=label + "_s", align_bytes=64)
             nc.vector.quantize_mx(out=codes[:].bitcast(FP8X4), scales=scales[:], in_=grouped_flat)
             return codes, scales
 
         def turn_w(w_raw, g):
-            w_g = grp.tile([P, 4, P, 4], BF16, tag="grp", name="w_g", align_bytes=64)
-            for b in range(2):
-                empty(turn_head(w_raw[:, g, 2 * b : 2 * b + 2, :]), w_g[:, 2 * b : 2 * b + 2, :, :].bitcast(F32))
+            w_g = grp.tile([P, PACK, P, PACK], BF16, tag="grp", name="w_g", align_bytes=64)
+            for t in range(0, PACK, 2):
+                empty(turn([w_raw[:, g, t, :], w_raw[:, g, t + 1, :]]), w_g[:, t : t + 2, :, :].bitcast(F32))
             return w_g
 
         def quant_w(w_g, label):
-            return quantize(w_g[:].rearrange("p t m j -> p (t m j)"), 2048, keep, label)
+            return quantize(w_g[:].rearrange("p t m j -> p (t m j)"), PACK * K_PASS, keep, label)
 
         def turn_f(g):
-            return [turn_head(f_raw[:, g, 2 * b : 2 * b + 2, :]) for b in range(2)]
+            return [turn([f_raw[:, g, 2 * h, :], f_raw[:, g, 2 * h + 1, :]]) for h in range(2)]
 
         def stage1(g, which, w_q, dst):
             codes, scales = w_q
-            for t in range(4):
-                ps = psum.tile([P, B], BANK_DT, tag="bank", name="ps1")
-                cols = slice(P * t, P * (t + 1))
+            for t in range(PACK):
+                ps = psum.tile([P, B], STAGE1_PSUM_DT, tag="bank", name="ps1")
+                slot = slice(P * t, P * (t + 1))
                 nc.tensor.matmul_mx(
                     out=ps[:],
-                    lhsT=codes[:, cols].bitcast(FP8X4),
-                    lhsT_scale=scales[:, cols],
+                    lhsT=codes[:, slot].bitcast(FP8X4),
+                    lhsT_scale=scales[:, slot],
                     rhs=y_c[:].bitcast(FP8X4),
                     rhs_scale=y_s[:],
                     start=True,
@@ -152,9 +136,9 @@ def tile_smcrossbaby_1_pb_kernel(tc, y2, first, w_second, b_second, w_int, b_int
         def gate_mul(s_sb, f_banks):
             prods = []
             for h in range(2):
-                sf = mid.tile([P, 256, 4], F32, tag="sf", name="sf")
+                sf = mid.tile([P, TOK_HALF, PACK], F32, tag="sf", name="sf")
                 for x in range(2):
-                    toks = slice(256 * h + P * x, 256 * h + P * (x + 1))
+                    toks = slice(TOK_HALF * h + P * x, TOK_HALF * h + P * (x + 1))
                     nc.vector.tensor_tensor(
                         out=sf[:, P * x : P * (x + 1), :].rearrange("p r (u e) -> p r u e", e=2),
                         in0=s_sb[:, :, toks].rearrange("p (u e) r -> p r u e", e=2),
@@ -165,9 +149,9 @@ def tile_smcrossbaby_1_pb_kernel(tc, y2, first, w_second, b_second, w_int, b_int
             return prods
 
         def gate_add(prods, i_sb):
-            z_g = mid.tile([P, B, 4], BF16, tag="z_g", name="z_g", align_bytes=64)
+            z_g = mid.tile([P, B, PACK], BF16, tag="z_g", name="z_g", align_bytes=64)
             for h in range(2):
-                toks = slice(256 * h, 256 * (h + 1))
+                toks = slice(TOK_HALF * h, TOK_HALF * (h + 1))
                 nc.vector.tensor_tensor(out=z_g[:, toks, :], in0=prods[h][:], in1=i_sb[:, :, toks].rearrange("p t n -> p n t"), op=ALU.add)
             return z_g
 
@@ -175,56 +159,55 @@ def tile_smcrossbaby_1_pb_kernel(tc, y2, first, w_second, b_second, w_int, b_int
             codes = keep.tile([P, B], U32, name=label + "_c", align_bytes=64)
             scales = keep.tile([P, B], U8, name=label + "_s", align_bytes=64)
             for h in range(2):
-                toks = slice(256 * h, 256 * (h + 1))
+                toks = slice(TOK_HALF * h, TOK_HALF * (h + 1))
                 nc.vector.quantize_mx(
                     out=codes[:, toks].bitcast(FP8X4), scales=scales[:, toks], in_=z_g[:, toks, :].rearrange("p n t -> p (n t)")
                 )
             return codes, scales
 
-        sorted_wo = {}
-
-        def sort_wo(c):
-            if SORT_FROM <= c < N_CHUNKS:
-                sorted_wo[c] = [sort_words(wo_raw[c][:, j, :, :], j >= 3) for j in range(4)]
-
         def turn_wo(c):
-            wo_g = grp.tile([P, 2, CHUNK, 4], BF16, tag="grp", name="wo_g", align_bytes=64)
-            for j in range(4):
-                xt = turn(wo_raw[c][:, j, :, :], sorted_wo[c][j] if c in sorted_wo else None)
+            wo_g = grp.tile([P, PASSES, CHUNK, PACK], BF16, tag="grp", name="wo_g", align_bytes=64)
+            for j in range(ROW_TILES):
+                xt = turn([wo_raw[c][:, j, 0:K_PASS], wo_raw[c][:, j, K_PASS:M]])
                 empty(xt, wo_g[:, :, P * j : P * (j + 1), :].bitcast(F32))
             return wo_g
 
         def quant_wo(wo_g):
-            return quantize(wo_g[:].rearrange("p g v t -> p (g v t)"), 8 * CHUNK, wcod, "wo")
+            return quantize(wo_g[:].rearrange("p g v t -> p (g v t)"), PACK * PASSES * CHUNK, wcod, "wo")
 
         def stage2(c, wo_q):
             codes, scales = wo_q
-            for m in range(4):
+            for a in range(TOK_TILES):
                 acc = psum.tile([P, CHUNK], F32, tag="bank", name="acc")
-                toks = slice(P * m, P * (m + 1))
-                for g in range(2):
-                    cols = slice(CHUNK * g, CHUNK * (g + 1))
+                toks = slice(P * a, P * (a + 1))
+                for g in range(PASSES):
+                    pass_cols = slice(CHUNK * g, CHUNK * (g + 1))
                     nc.tensor.matmul_mx(
                         out=acc[:],
                         lhsT=z_q[g][0][:, toks].bitcast(FP8X4),
                         lhsT_scale=z_q[g][1][:, toks],
-                        rhs=codes[:, cols].bitcast(FP8X4),
-                        rhs_scale=scales[:, cols],
+                        rhs=codes[:, pass_cols].bitcast(FP8X4),
+                        rhs_scale=scales[:, pass_cols],
                         start=(g == 0),
-                        stop=(g == 1),
+                        stop=(g == PASSES - 1),
                     )
                 o_sb = outp.tile([P, CHUNK], F32, tag="o_sb", name="o_sb")
                 vcols = slice(CHUNK * c, CHUNK * (c + 1))
-                nc.vector.tensor_tensor(out=o_sb[:], in0=acc[:], in1=bias_bc[:, vcols], op=ALU.add)
+                if c >= SHARED_FROM and a == SHARED_TILE:
+                    sums = outp.tile([P, CHUNK], F32, tag="sums", name="sums", bufs=2)
+                    nc.scalar.copy(out=sums[:], in_=acc[:])
+                    nc.gpsimd.tensor_tensor(out=o_sb[:], in0=sums[:], in1=bias_bc[:, vcols], op=ALU.add)
+                else:
+                    nc.vector.tensor_tensor(out=o_sb[:], in0=acc[:], in1=bias_bc[:, vcols], op=ALU.add)
                 nc.sync.dma_start(out=out[toks, vcols], in_=o_sb[:])
 
-        y_g = grp.tile([P, B, 4], BF16, tag="grp", name="y_g", align_bytes=64)
-        for b in range(2):
+        y_g = grp.tile([P, B, PACK], BF16, tag="grp", name="y_g", align_bytes=64)
+        for h in range(2):
             empty(
-                turn_head(y_raw[:, 2 * b : 2 * b + 2, :]),
-                y_g[:, 256 * b : 256 * (b + 1), :].bitcast(F32).rearrange("p (x r) u -> p x r u", x=2),
+                turn([y_raw[:, 2 * h, :], y_raw[:, 2 * h + 1, :]]),
+                y_g[:, TOK_HALF * h : TOK_HALF * (h + 1), :].bitcast(F32).rearrange("p (x r) u -> p x r u", x=2),
             )
-        y_c, y_s = quantize(y_g[:].rearrange("p n t -> p (n t)"), 4 * B, keep, "y")
+        y_c, y_s = quantize(y_g[:].rearrange("p n t -> p (n t)"), PACK * B, keep, "y")
 
         ws_g0 = turn_w(ws_raw, 0)
         wi_g0 = turn_w(wi_raw, 0)
@@ -232,8 +215,8 @@ def tile_smcrossbaby_1_pb_kernel(tc, y2, first, w_second, b_second, w_int, b_int
         wi_q0 = quant_w(wi_g0, "wi0")
         ws_g1 = turn_w(ws_raw, 1)
         wi_g1 = turn_w(wi_raw, 1)
-        s0 = mid.tile([P, 4, B], F32, tag="s_sb", name="s_sb")
-        i0 = mid.tile([P, 4, B], F32, tag="i_sb", name="i_sb")
+        s0 = mid.tile([P, PACK, B], F32, tag="s_sb", name="s_sb")
+        i0 = mid.tile([P, PACK, B], F32, tag="i_sb", name="i_sb")
         stage1(0, 0, ws_q0, s0)
         stage1(0, 1, wi_q0, i0)
         f_banks0 = turn_f(0)
@@ -241,10 +224,9 @@ def tile_smcrossbaby_1_pb_kernel(tc, y2, first, w_second, b_second, w_int, b_int
         wi_q1 = quant_w(wi_g1, "wi1")
         prods0 = gate_mul(s0, f_banks0)
         wo_qs = {}
-        sort_wo(0)
         wo_g0 = turn_wo(0)
-        s1 = mid.tile([P, 4, B], F32, tag="s_sb", name="s_sb")
-        i1 = mid.tile([P, 4, B], F32, tag="i_sb", name="i_sb")
+        s1 = mid.tile([P, PACK, B], F32, tag="s_sb", name="s_sb")
+        i1 = mid.tile([P, PACK, B], F32, tag="i_sb", name="i_sb")
         stage1(1, 0, ws_q1, s1)
         stage1(1, 1, wi_q1, i1)
         f_banks1 = turn_f(1)
@@ -254,12 +236,9 @@ def tile_smcrossbaby_1_pb_kernel(tc, y2, first, w_second, b_second, w_int, b_int
         z_g1 = gate_add(prods1, i1)
         z_q.append(quant_z(z_g1, "z1"))
         wo_qs[0] = quant_wo(wo_g0)
-        for c in range(1, AHEAD + 1):
-            sort_wo(c)
         for c in range(1, AHEAD):
             wo_qs[c] = quant_wo(turn_wo(c))
         for c in range(N_CHUNKS):
-            sort_wo(c + AHEAD + 1)
             stage2(c, wo_qs[c])
             if c + AHEAD < N_CHUNKS:
                 wo_qs[c + AHEAD] = quant_wo(turn_wo(c + AHEAD))

from contextlib import ExitStack

import concourse.mybir as mybir
from concourse.masks import make_identity

B, E, M, V = 512, 512, 1024, 4096
FLOPS = 2 * B * E * M * 2 + 2 * B * M * V

F32 = mybir.dt.float32
BF16 = mybir.dt.bfloat16
U32 = mybir.dt.uint32
U8 = mybir.dt.uint8
FP8X4 = mybir.dt.float8_e4m3fn_x4
ACT = mybir.ActivationFunctionType
ALU = mybir.AluOpType

P = 128
PACK = 4
K_PASS = P * PACK
PASSES = M // K_PASS
STAGE1_PSUM_DT = F32
CHUNK = 512
N_CHUNKS = V // CHUNK
ROW_TILES = CHUNK // P
TOK_TILES = B // P
TOK_HALF = B // 2
AHEAD = 4
SHARED_FROM = N_CHUNKS - AHEAD
SHARED_TILE = 1


def tile_smcrossbaby_1_pb_kernel(tc, y2, first, w_second, b_second, w_int, b_int, w_out, b_out, out):
    nc = tc.nc
    with ExitStack() as ctx:
        const = ctx.enter_context(tc.tile_pool(name="const", bufs=1))
        raw = ctx.enter_context(tc.tile_pool(name="raw", bufs=8))
        grp = ctx.enter_context(tc.tile_pool(name="grp", bufs=4))
        keep = ctx.enter_context(tc.tile_pool(name="keep", bufs=1))
        wcod = ctx.enter_context(tc.tile_pool(name="wcod", bufs=AHEAD + 1))
        mid = ctx.enter_context(tc.tile_pool(name="mid", bufs=2))
        outp = ctx.enter_context(tc.tile_pool(name="outp", bufs=12))
        psum = ctx.enter_context(tc.psum_pool(name="psum", bufs=8))
        ctx.enter_context(tc.manual_schedule(engines={mybir.EngineType.PE}))

        bcol = const.tile([P, 2, PASSES, PACK], F32, name="bcol")
        for which, vec in enumerate((b_second, b_int)):
            bcol_raw = const.tile([P, PASSES, PACK], BF16, name="bcol_raw%d" % which)
            nc.scalar.dma_start(out=bcol_raw[:], in_=vec.rearrange("(g p t) -> p g t", g=PASSES, t=PACK))
            nc.vector.tensor_copy(out=bcol[:, which, :, :], in_=bcol_raw[:])
        y_raw = raw.tile([P, TOK_TILES, E], BF16, tag="raw", name="y_raw")
        y_view = y2.rearrange("(a p) k -> p a k", p=P)
        nc.sync.dma_start(out=y_raw[:, 0:2, :], in_=y_view[:, 0:2, :])
        nc.sync.dma_start(out=y_raw[:, 2:4, :], in_=y_view[:, 2:4, :])
        ws_raw = raw.tile([P, PASSES, PACK, E], BF16, tag="raw", name="ws_raw")
        wi_raw = raw.tile([P, PASSES, PACK, E], BF16, tag="raw", name="wi_raw")
        f_raw = raw.tile([P, PASSES, TOK_TILES, K_PASS], BF16, tag="raw", name="f_raw")
        for g in range(PASSES):
            rows = slice(K_PASS * g, K_PASS * (g + 1))
            nc.sync.dma_start(out=ws_raw[:, g, :, :], in_=w_second[rows, :].rearrange("(m t) k -> m t k", t=PACK))
            nc.sync.dma_start(out=wi_raw[:, g, :, :], in_=w_int[rows, :].rearrange("(m t) k -> m t k", t=PACK))
        for g in range(PASSES):
            chans = slice(K_PASS * g, K_PASS * (g + 1))
            nc.sync.dma_start(out=f_raw[:, g, :, :], in_=first[:, chans].rearrange("(a p) c -> p a c", p=P))
        bias_bc = const.tile([P, V], BF16, name="bias_bc")

        def load_bias(c):
            vcols = slice(CHUNK * c, CHUNK * (c + 1))
            nc.sync.dma_start(out=bias_bc[:, vcols], in_=b_out[vcols].partition_broadcast(P))

        wo_raw = []
        for c in range(N_CHUNKS):
            chunk_raw = raw.tile([P, ROW_TILES, M], BF16, tag="raw", name="wo_raw")
            nc.sync.dma_start(out=chunk_raw[:], in_=w_out[CHUNK * c : CHUNK * (c + 1), :].rearrange("(j p) k -> p j k", p=P))
            wo_raw.append(chunk_raw)
            if c >= 2:
                load_bias(c - 2)
        load_bias(N_CHUNKS - 2)
        load_bias(N_CHUNKS - 1)

        ident = const.tile([P, P], F32, name="ident")
        make_identity(nc, ident[:])
        warm = const.tile([P, 1], F32, name="warm")
        nc.vector.memset(warm[:], 0.0)
        warm2 = const.tile([P, 1], F32, name="warm2")
        nc.scalar.activation(out=warm2[:], in_=warm[:], func=ACT.Relu)

        def turn(srcs):
            xt = psum.tile([P, 2, 2, P], F32, tag="bank", name="xt")
            for x in range(2):
                words = srcs[x].bitcast(F32)
                for u in range(2):
                    nc.tensor.transpose(xt[:, x, u, :], words[:, u::2], ident[:])
            return xt

        def empty(xt, dst_words):
            nc.scalar.copy(out=dst_words, in_=xt[:].rearrange("p x u r -> p x r u"))

        def quantize(grouped_flat, width, pool, label):
            codes = pool.tile([P, width // PACK], U32, name=label + "_c", tag=label + "_c", align_bytes=64)
            scales = pool.tile([P, width // PACK], U8, name=label + "_s", tag=label + "_s", align_bytes=64)
            nc.vector.quantize_mx(out=codes[:].bitcast(FP8X4), scales=scales[:], in_=grouped_flat)
            return codes, scales

        def turn_w(w_raw, g):
            w_g = grp.tile([P, PACK, P, PACK], BF16, tag="grp", name="w_g", align_bytes=64)
            for t in range(0, PACK, 2):
                empty(turn([w_raw[:, g, t, :], w_raw[:, g, t + 1, :]]), w_g[:, t : t + 2, :, :].bitcast(F32))
            return w_g

        def quant_w(w_g, label):
            return quantize(w_g[:].rearrange("p t m j -> p (t m j)"), PACK * K_PASS, keep, label)

        def turn_f(g):
            return [turn([f_raw[:, g, 2 * h, :], f_raw[:, g, 2 * h + 1, :]]) for h in range(2)]

        def stage1(g, which, w_q, dst):
            codes, scales = w_q
            for t in range(PACK):
                ps = psum.tile([P, B], STAGE1_PSUM_DT, tag="bank", name="ps1")
                slot = slice(P * t, P * (t + 1))
                nc.tensor.matmul_mx(
                    out=ps[:],
                    lhsT=codes[:, slot].bitcast(FP8X4),
                    lhsT_scale=scales[:, slot],
                    rhs=y_c[:].bitcast(FP8X4),
                    rhs_scale=y_s[:],
                    start=True,
                    stop=True,
                )
                b_ap = bcol[:, which, g, t : t + 1]
                if g == 0 and which == 1 and t % 2 == 0:
                    nc.vector.tensor_scalar(out=dst[:, t, :], in0=ps[:], scalar1=b_ap, scalar2=0.0, op0=ALU.add, op1=ALU.max)
                else:
                    nc.scalar.activation(out=dst[:, t, :], in_=ps[:], func=ACT.Relu, bias=b_ap, scale=1.0)

        def gate_mul(s_sb, f_banks):
            prods = []
            for h in range(2):
                sf = mid.tile([P, TOK_HALF, PACK], F32, tag="sf", name="sf")
                for x in range(2):
                    toks = slice(TOK_HALF * h + P * x, TOK_HALF * h + P * (x + 1))
                    nc.vector.tensor_tensor(
                        out=sf[:, P * x : P * (x + 1), :].rearrange("p r (u e) -> p r u e", e=2),
                        in0=s_sb[:, :, toks].rearrange("p (u e) r -> p r u e", e=2),
                        in1=f_banks[h][:, x, :, :].bitcast(BF16).rearrange("p u (r e) -> p r u e", e=2),
                        op=ALU.mult,
                    )
                prods.append(sf)
            return prods

        def gate_add(prods, i_sb):
            z_g = mid.tile([P, B, PACK], BF16, tag="z_g", name="z_g", align_bytes=64)
            for h in range(2):
                toks = slice(TOK_HALF * h, TOK_HALF * (h + 1))
                nc.vector.tensor_tensor(out=z_g[:, toks, :], in0=prods[h][:], in1=i_sb[:, :, toks].rearrange("p t n -> p n t"), op=ALU.add)
            return z_g

        def quant_z(z_g, label):
            codes = keep.tile([P, B], U32, name=label + "_c", align_bytes=64)
            scales = keep.tile([P, B], U8, name=label + "_s", align_bytes=64)
            for h in range(2):
                toks = slice(TOK_HALF * h, TOK_HALF * (h + 1))
                nc.vector.quantize_mx(
                    out=codes[:, toks].bitcast(FP8X4), scales=scales[:, toks], in_=z_g[:, toks, :].rearrange("p n t -> p (n t)")
                )
            return codes, scales

        def turn_wo(c):
            wo_g = grp.tile([P, PASSES, CHUNK, PACK], BF16, tag="grp", name="wo_g", align_bytes=64)
            for j in range(ROW_TILES):
                xt = turn([wo_raw[c][:, j, 0:K_PASS], wo_raw[c][:, j, K_PASS:M]])
                empty(xt, wo_g[:, :, P * j : P * (j + 1), :].bitcast(F32))
            return wo_g

        def quant_wo(wo_g):
            return quantize(wo_g[:].rearrange("p g v t -> p (g v t)"), PACK * PASSES * CHUNK, wcod, "wo")

        def stage2(c, wo_q):
            codes, scales = wo_q
            for a in range(TOK_TILES):
                acc = psum.tile([P, CHUNK], F32, tag="bank", name="acc")
                toks = slice(P * a, P * (a + 1))
                for g in range(PASSES):
                    pass_cols = slice(CHUNK * g, CHUNK * (g + 1))
                    nc.tensor.matmul_mx(
                        out=acc[:],
                        lhsT=z_q[g][0][:, toks].bitcast(FP8X4),
                        lhsT_scale=z_q[g][1][:, toks],
                        rhs=codes[:, pass_cols].bitcast(FP8X4),
                        rhs_scale=scales[:, pass_cols],
                        start=(g == 0),
                        stop=(g == PASSES - 1),
                    )
                o_sb = outp.tile([P, CHUNK], F32, tag="o_sb", name="o_sb")
                vcols = slice(CHUNK * c, CHUNK * (c + 1))
                if c >= SHARED_FROM and a == SHARED_TILE:
                    sums = outp.tile([P, CHUNK], F32, tag="sums", name="sums", bufs=2)
                    nc.scalar.copy(out=sums[:], in_=acc[:])
                    nc.gpsimd.tensor_tensor(out=o_sb[:], in0=sums[:], in1=bias_bc[:, vcols], op=ALU.add)
                else:
                    nc.vector.tensor_tensor(out=o_sb[:], in0=acc[:], in1=bias_bc[:, vcols], op=ALU.add)
                nc.sync.dma_start(out=out[toks, vcols], in_=o_sb[:])

        y_g = grp.tile([P, B, PACK], BF16, tag="grp", name="y_g", align_bytes=64)
        for h in range(2):
            empty(
                turn([y_raw[:, 2 * h, :], y_raw[:, 2 * h + 1, :]]),
                y_g[:, TOK_HALF * h : TOK_HALF * (h + 1), :].bitcast(F32).rearrange("p (x r) u -> p x r u", x=2),
            )
        y_c, y_s = quantize(y_g[:].rearrange("p n t -> p (n t)"), PACK * B, keep, "y")

        ws_g0 = turn_w(ws_raw, 0)
        wi_g0 = turn_w(wi_raw, 0)
        ws_q0 = quant_w(ws_g0, "ws0")
        wi_q0 = quant_w(wi_g0, "wi0")
        ws_g1 = turn_w(ws_raw, 1)
        wi_g1 = turn_w(wi_raw, 1)
        s0 = mid.tile([P, PACK, B], F32, tag="s_sb", name="s_sb")
        i0 = mid.tile([P, PACK, B], F32, tag="i_sb", name="i_sb")
        stage1(0, 0, ws_q0, s0)
        stage1(0, 1, wi_q0, i0)
        f_banks0 = turn_f(0)
        ws_q1 = quant_w(ws_g1, "ws1")
        wi_q1 = quant_w(wi_g1, "wi1")
        prods0 = gate_mul(s0, f_banks0)
        wo_qs = {}
        wo_g0 = turn_wo(0)
        s1 = mid.tile([P, PACK, B], F32, tag="s_sb", name="s_sb")
        i1 = mid.tile([P, PACK, B], F32, tag="i_sb", name="i_sb")
        stage1(1, 0, ws_q1, s1)
        stage1(1, 1, wi_q1, i1)
        f_banks1 = turn_f(1)
        z_g0 = gate_add(prods0, i0)
        prods1 = gate_mul(s1, f_banks1)
        z_q = [quant_z(z_g0, "z0")]
        z_g1 = gate_add(prods1, i1)
        z_q.append(quant_z(z_g1, "z1"))
        wo_qs[0] = quant_wo(wo_g0)
        for c in range(1, AHEAD):
            wo_qs[c] = quant_wo(turn_wo(c))
        for c in range(N_CHUNKS):
            stage2(c, wo_qs[c])
            if c + AHEAD < N_CHUNKS:
                wo_qs[c + AHEAD] = quant_wo(turn_wo(c + AHEAD))
